import numpy as np
import ml_dtypes


def mxq(x, axis, fmt="e4m3"):
    dtype, down = {"e4m3": (ml_dtypes.float8_e4m3fn, 7), "e5m2": (ml_dtypes.float8_e5m2, 14)}[fmt]
    v = np.moveaxis(np.asarray(x, np.float32).astype(ml_dtypes.bfloat16).astype(np.float64), axis, -1)
    blocks = v.reshape(v.shape[:-1] + (-1, 32))
    amax = np.abs(blocks).max(-1, keepdims=True)
    byte = np.maximum(np.where(amax > 0, np.frexp(amax)[1] - 1 + 127, 0) - down, 1)
    scale = np.exp2(byte - 127.0)
    codes = (blocks / scale).astype(np.float32).astype(dtype).astype(np.float64)
    return np.moveaxis((codes * scale).reshape(v.shape), -1, axis)


WIDE = False


def mx_kscale(k):
    if not WIDE:
        return np.ones(k)
    levels = np.array([18, -18])
    if k % 512:
        return np.exp2(np.random.permutation(np.resize(levels, k // 32))).repeat(32)
    a = np.empty((k // 512, 16))
    for p in range(k // 512):
        a[p, :8] = np.random.permutation(np.resize(levels, 8))
        for g in range(8):
            far = levels[np.abs(levels - a[p, g]) >= 10]
            a[p, g + 8] = far[np.random.randint(len(far))]
    return np.exp2(a.ravel()).repeat(32)


BF16 = ml_dtypes.bfloat16


def bf(x):
    return np.asarray(x, np.float32).astype(BF16)


def f64(x):
    return np.asarray(x).astype(np.float64)


B, D = 1024, 1024


def setup_inputs():
    s = np.minimum(mx_kscale(B), 1.0)[:, None]
    u = mx_kscale(D)
    v = mx_kscale(D)
    x0 = bf(np.random.standard_normal((B, D)))
    w_j0 = bf(np.random.standard_normal((D, D)) / np.sqrt(D))
    b_j = bf(np.random.standard_normal(D) * 0.3)
    w_i0 = bf(np.random.standard_normal((D, D)) / np.sqrt(D))
    g = bf(np.random.standard_normal((B, D)) * np.exp2(np.random.randint(-6, 1, (B, 1))) * 4.0 / s * u)
    phi = np.tanh(f64(x0)) @ f64(w_j0).T + f64(b_j)
    return {"x": bf(f64(x0) * s),
            "w_j": bf(f64(w_j0) / v[:, None]),
            "b_j": b_j,
            "w_i": bf(f64(w_i0) * v / u[:, None]),
            "phi": np.asarray(phi, np.float32),
            "grad_out": g}


def reference(x, w_j, b_j, w_i, phi, grad_out):
    t = np.tanh(f64(x))
    gate = 1.0 - t * t
    dh = mxq(f64(grad_out), 1, "e5m2") @ mxq(f64(w_i), 0, "e4m3")
    dz1 = dh * gate
    dt = mxq(dz1, 1, "e5m2") @ mxq(f64(w_j), 0, "e4m3")
    dx = gate * (dt - 2.0 * t * f64(phi) * dh)
    dw_j = mxq(dz1, 0, "e5m2").T @ mxq(t, 0, "e4m3")
    return dx, dw_j

@@ -1,0 +1,398 @@
+from contextlib import ExitStack
+
+import concourse.mybir as mybir
+from concourse.masks import make_identity
+
+F32 = mybir.dt.float32
+BF16 = mybir.dt.bfloat16
+U32 = mybir.dt.uint32
+U8 = mybir.dt.uint8
+E4M3 = mybir.dt.float8_e4m3fn_x4
+E5M2 = mybir.dt.float8_e5m2_x4
+ALU = mybir.AluOpType
+ACT = mybir.ActivationFunctionType
+
+FLOPS = 3 * 2 * 1024**3
+BYTES = 1024 * 1024 * (4 * 2 + 4 + 2 * 4)
+
+P = 128
+J = 4
+H = 512
+D = 1024
+
+
+def tile_inimnetdisc_pc_v_kernel(tc, x, w_j, b_j, w_i, phi, grad_out, out_0, out_1):
+    nc = tc.nc
+    rows = lambda ap: ap.rearrange("(g p j) w -> g p j w", p=P, j=J)
+    x_v, wj_v, wi_v, phi_v, go_v, dx_v = rows(x), rows(w_j), rows(w_i), rows(phi), rows(grad_out), rows(out_0)
+    with ExitStack() as ctx:
+        const = ctx.enter_context(tc.tile_pool(name="const", bufs=1))
+        keep = ctx.enter_context(tc.tile_pool(name="keep", bufs=1))
+        raw = ctx.enter_context(tc.tile_pool(name="raw", bufs=4))
+        work = ctx.enter_context(tc.tile_pool(name="work", bufs=6))
+        psum = ctx.enter_context(tc.psum_pool(name="psum", bufs=2))
+
+        id32 = const.tile([P, P], F32, name="id32")
+        id16 = const.tile([P, P], BF16, name="id16")
+        make_identity(nc, id32[:])
+        make_identity(nc, id16[:])
+        warm = const.tile([P, 8], F32, name="warm")
+        nc.vector.memset(warm[:], 0.0)
+
+        def operand(name):
+            codes = keep.tile([P, 2, D], U32, name=name + "_c", align_bytes=64)
+            scales = keep.tile([P, 2, D], U8, name=name + "_s", align_bytes=64)
+            return codes, scales
+
+        wi_q, wj_q, t_q = operand("wi"), operand("wj"), operand("t")
+        g_q, dzh_q, dzt_q = operand("g"), operand("dzh"), operand("dzt")
+
+        def quant(dst, c, cols, src, fmt):
+            nc.vector.quantize_mx(out=dst[0][:, c, cols].bitcast(fmt), scales=dst[1][:, c, cols], in_=src)
+
+        def mx(out, lhs, c, m0, fl, rhs, cr, n0, fr, start, stop):
+            nc.tensor.matmul_mx(
+                out=out,
+                lhsT=lhs[0][:, c, m0 : m0 + P].bitcast(fl),
+                lhsT_scale=lhs[1][:, c, m0 : m0 + P],
+                rhs=rhs[0][:, cr, n0 : n0 + H].bitcast(fr),
+                rhs_scale=rhs[1][:, cr, n0 : n0 + H],
+                start=start,
+                stop=stop,
+            )
+
+        def half(i):
+            return slice(i * H, (i + 1) * H)
+
+        with tc.manual_schedule():
+            xr, phr, s, t32, dzb = {}, {}, {}, {}, {}
+
+            def load_x(g, h):
+                xr[g, h] = keep.tile([P, J, H], BF16, name=f"x{g}{h}")
+                nc.sync.dma_start(out=xr[g, h][:], in_=x_v[g][:, :, half(h)])
+
+            def load_phi(g, h):
+                phr[g, h] = keep.tile([P, J, H], F32, name=f"phi{g}{h}")
+                nc.sync.dma_start(out=phr[g, h][:], in_=phi_v[g][:, :, half(h)])
+
+            wir, wjr, gr = {}, {}, {}
+
+            def load_wi(h, c):
+                if c == 0:
+                    wir[h] = raw.tile([P, 2, J, H], BF16, name="rawt")
+                nc.sync.dma_start(out=wir[h][:, c], in_=wi_v[c][:, :, half(h)])
+
+            def load_g(g):
+                gr[g] = raw.tile([P, J, D], BF16, name="rawt")
+                nc.sync.dma_start(out=gr[g][:], in_=go_v[g])
+
+            def load_wj(c):
+                wjr[c] = raw.tile([P, J, D], BF16, name="rawt")
+                nc.sync.dma_start(out=wjr[c][:], in_=wj_v[c])
+
+            def tanh(g, h):
+                t32[g, h] = work.tile([P, J, H], F32, name="t32", bufs=2)
+                nc.scalar.activation(t32[g, h][:], xr[g, h][:], ACT.Tanh)
+
+            def square(g, h, js):
+                if js[0] == 0:
+                    s[g, h] = keep.tile([P, J, H], F32, name=f"s{g}{h}")
+                nc.scalar.activation(s[g, h][:, js[0] : js[-1] + 1], t32[g, h][:, js[0] : js[-1] + 1], ACT.Square)
+
+            def grouped():
+                return work.tile([P, H, J], BF16, name="grouped", align_bytes=64)
+
+            def flat(t):
+                return t[:].rearrange("p w j -> p (w j)")
+
+            tb = {}
+
+            def t_group(g, h):
+                tb[g, h] = grouped()
+                nc.scalar.activation(tb[g, h][:], xr[g, h][:].rearrange("p j w -> p w j"), ACT.Tanh)
+
+            def t_quant(g, h):
+                quant(t_q, g, half(h), flat(tb[g, h]), E4M3)
+
+            def copier(eng):
+                return nc.vector.tensor_copy if eng == "v" else nc.scalar.copy
+
+            wib = {}
+
+            def wi_group(h, c, eng):
+                wib[h, c] = grouped()
+                copier(eng)(
+                    out=wib[h, c][:].rearrange("p (c i) t -> p c t i", i=4),
+                    in_=wir[h][:, c].rearrange("p t (c i) -> p c t i", i=4),
+                )
+
+            def wi_quant(h, c):
+                quant(wi_q, c, half(h), flat(wib[h, c]), E4M3)
+
+            gt = {}
+
+            def transposes(src32, col0):
+                banks = []
+                for b in range(2):
+                    bank = psum.tile([P, 2, 2, P], F32, name="tr", bufs=2)
+                    for jj in range(2):
+                        for u in range(2):
+                            nc.tensor.transpose(bank[:, jj, u, :], src32[:, 2 * b + jj, col0 + u : col0 + 2 * P : 2], id32[:])
+                    banks.append(bank)
+                return banks
+
+            def untranspose(eng, dst, bank, b):
+                o = dst[:].rearrange("p w j -> p (w j)").bitcast(F32).rearrange("p (b a r u) -> p b a r u", b=2, a=2, u=2)[:, b]
+                i = bank[:].rearrange("p a u r -> p a r u")
+                copier(eng)(out=o, in_=i)
+
+            def g_turn(g, c, engs):
+                gt[g, c] = grouped()
+                words = gr[g][:].rearrange("p j w -> p (j w)").bitcast(F32).rearrange("p (j w) -> p j w", j=J)
+                banks = transposes(words, 256 * c)
+                for b in range(2):
+                    untranspose(engs[b], gt[g, c], banks[b], b)
+
+            def g_quant(g, c):
+                quant(g_q, c, half(g), flat(gt[g, c]), E5M2)
+
+            dh = {}
+
+            def dh_mm(g, h, js):
+                for j in js:
+                    bank = psum.tile([P, H], F32, name="acc", bufs=6)
+                    for c in range(2):
+                        mx(bank[:], g_q, c, g * H + j * P, E5M2, wi_q, c, h * H, E4M3, c == 0, c == 1)
+                    dh[g, h, j] = bank
+
+            def dz(g, h, js):
+                if js[0] == 0:
+                    dzb[g, h] = work.tile([P, J, H], BF16, name="dz", bufs=2)
+                for j in js:
+                    nc.vector.scalar_tensor_tensor(
+                        out=dzb[g, h][:, j, :], in0=s[g, h][:, j, :], scalar=1.0, in1=dh[g, h, j][:], op0=ALU.subtract, op1=ALU.mult
+                    )
+
+            def a(g, h, js, eng):
+                for j in js:
+                    e = nc.gpsimd if eng == "g" else nc.vector
+                    e.tensor_tensor(out=phr[g, h][:, j, :], in0=t32[g, h][:, j, :], in1=phr[g, h][:, j, :], op=ALU.mult)
+
+            def u(g, h, js):
+                for j in js:
+                    nc.vector.tensor_tensor(out=phr[g, h][:, j, :], in0=dh[g, h, j][:], in1=phr[g, h][:, j, :], op=ALU.mult)
+
+            dzTb, dzib = {}, {}
+
+            def dz_turn(g, h, engs):
+                dzTb[g, h] = grouped()
+                words = dzb[g, h][:].rearrange("p j w -> p (j w)").bitcast(F32).rearrange("p (j w) -> p j w", j=J)
+                banks = transposes(words, 0)
+                for b in range(2):
+                    untranspose(engs[b], dzTb[g, h], banks[b], b)
+
+            def move(dst, src, engs):
+                for b in range(2):
+                    bank = psum.tile([P, 2 * P, J], BF16, name="tr", bufs=2)
+                    for k in range(2):
+                        w0 = b * 256 + k * P
+                        nc.tensor.matmul(
+                            bank[:, k * P : (k + 1) * P, :],
+                            lhsT=id16[:],
+                            rhs=src[:, :, w0 : w0 + P].rearrange("p j w -> p w j"),
+                            start=True,
+                            stop=True,
+                        )
+                    copier(engs[b])(out=dst[:, b * 256 : b * 256 + 256, :], in_=bank[:])
+
+            def dz_group(g, h, engs):
+                dzib[g, h] = grouped()
+                move(dzib[g, h], dzb[g, h], engs)
+
+            def dzT_quant(g, h):
+                quant(dzh_q, h, half(g), flat(dzTb[g, h]), E5M2)
+
+            def dzi_quant(g, h):
+                quant(dzt_q, g, half(h), flat(dzib[g, h]), E5M2)
+
+            wjb = {}
+
+            def wj_group(c, h, engs):
+                wjb[c, h] = grouped()
+                move(wjb[c, h], wjr[c][:, :, half(h)], engs)
+
+            def wj_quant(c, h):
+                quant(wj_q, c, half(h), flat(wjb[c, h]), E4M3)
+
+            dt = {}
+
+            def dt_mm(g, h, js):
+                for j in js:
+                    bank = psum.tile([P, H], F32, name="acc", bufs=6)
+                    for c in range(2):
+                        mx(bank[:], dzh_q, c, g * H + j * P, E5M2, wj_q, c, h * H, E4M3, c == 0, c == 1)
+                    dt[g, h, j] = bank
+
+            def v(g, h, j):
+                nc.vector.scalar_tensor_tensor(
+                    out=phr[g, h][:, j, :], in0=phr[g, h][:, j, :], scalar=2.0, in1=dt[g, h, j][:], op0=ALU.mult, op1=ALU.add
+                )
+
+            def o(g, h, j):
+                nc.vector.scalar_tensor_tensor(
+                    out=phr[g, h][:, j, :], in0=s[g, h][:, j, :], scalar=1.0, in1=phr[g, h][:, j, :], op0=ALU.subtract, op1=ALU.mult
+                )
+
+            def finish(g, h, j0):
+                v(g, h, j0)
+                v(g, h, j0 + 1)
+                o(g, h, j0)
+                o(g, h, j0 + 1)
+                nc.sync.dma_start(out=dx_v[g][:, j0 : j0 + 2, half(h)], in_=phr[g, h][:, j0 : j0 + 2, :])
+
+            def dw(m, engs):
+                stage = work.tile([P, D], F32, name="dw", bufs=3)
+                for h in range(2):
+                    bank = psum.tile([P, H], F32, name="acc", bufs=6)
+                    for g in range(2):
+                        mx(bank[:], dzt_q, g, m * P, E5M2, t_q, g, h * H, E4M3, g == 0, g == 1)
+                    if engs[h] == "s":
+                        nc.scalar.activation(stage[:, half(h)], bank[:], ACT.Copy, scale=-1.0)
+                    else:
+                        nc.vector.tensor_scalar(out=stage[:, half(h)], in0=bank[:], scalar1=-1.0, scalar2=None, op0=ALU.mult)
+                nc.sync.dma_start(out=out_1[m * P : (m + 1) * P, :], in_=stage[:])
+
+            LO, HI = (0, 1), (2, 3)
+            nc.scalar.activation(warm[:, 0:1], warm[:, 1:2], ACT.Tanh)
+            load_wi(1, 0)
+            wi_group(1, 0, "v")
+            load_g(0)
+            g_turn(0, 0, "ss")
+            g_turn(0, 1, "ss")
+            load_wi(0, 0)
+            wi_quant(1, 0)
+            wi_group(0, 0, "v")
+            g_quant(0, 0)
+            wi_quant(0, 0)
+            g_quant(0, 1)
+            load_x(0, 0)
+            load_wi(0, 1)
+            wi_group(0, 1, "v")
+            tanh(0, 0)
+            square(0, 0, LO)
+            load_wi(1, 1)
+            wi_group(1, 1, "v")
+            wi_quant(0, 1)
+            dh_mm(0, 0, LO)
+            load_x(1, 0)
+            load_phi(0, 0)
+            wi_quant(1, 1)
+            dh_mm(0, 0, HI)
+            load_g(1)
+            dz(0, 0, LO)
+            square(0, 0, HI)
+            a(0, 0, HI, "v")
+            dz(0, 0, HI)
+            tanh(1, 0)
+            a(0, 0, LO, "v")
+            square(1, 0, LO)
+            square(1, 0, HI)
+            load_x(0, 1)
+            g_turn(1, 0, "ss")
+            load_phi(1, 0)
+            load_phi(0, 1)
+            tanh(0, 1)
+            u(0, 0, LO)
+            g_turn(1, 1, "ss")
+            g_quant(1, 0)
+            load_phi(1, 1)
+            t_group(1, 0)
+            dz_turn(0, 0, "ss")
+            a(1, 0, HI, "v")
+            u(0, 0, HI)
+            a(0, 1, LO, "v")
+            g_quant(1, 1)
+            load_x(1, 1)
+            a(1, 0, LO, "v")
+            tanh(1, 1)
+            dh_mm(1, 0, LO)
+            dz_group(0, 0, "ss")
+            load_wj(1)
+            dh_mm(0, 1, LO)
+            a(0, 1, HI, "v")
+            u(1, 0, LO)
+            load_wj(0)
+            dz(1, 0, LO)
+            dh_mm(1, 0, HI)
+            dz(1, 0, HI)
+            a(1, 1, HI, "v")
+            dzi_quant(0, 0)
+            square(0, 1, LO)
+            wj_group(1, 1, "ss")
+            square(1, 1, LO)
+            dz_turn(1, 0, "ss")
+            square(0, 1, HI)
+            u(1, 0, HI)
+            u(0, 1, LO)
+            t_quant(1, 0)
+            dzT_quant(0, 0)
+            dz(0, 1, LO)
+            dz_group(1, 0, "ss")
+            dh_mm(0, 1, HI)
+            t_group(1, 1)
+            a(1, 1, LO, "v")
+            wj_group(0, 1, "ss")
+            dzT_quant(1, 0)
+            dz(0, 1, HI)
+            t_quant(1, 1)
+            dzi_quant(1, 0)
+            u(0, 1, HI)
+            wj_quant(1, 1)
+            dh_mm(1, 1, LO)
+            u(1, 1, LO)
+            square(1, 1, HI)
+            dh_mm(1, 1, HI)
+            u(1, 1, HI)
+            t_group(0, 1)
+            dz_turn(0, 1, "ss")
+            dz_group(0, 1, "ss")
+            wj_group(0, 0, "ss")
+            dz(1, 1, LO)
+            dzT_quant(0, 1)
+            wj_group(1, 0, "ss")
+            wj_quant(0, 1)
+            dt_mm(0, 1, LO)
+            t_group(0, 0)
+            t_quant(0, 1)
+            wj_quant(0, 0)
+            dz(1, 1, HI)
+            dz_group(1, 1, "ss")
+            wj_quant(1, 0)
+            finish(0, 1, 0)
+            dt_mm(0, 0, HI)
+            dz_turn(1, 1, "ss")
+            t_quant(0, 0)
+            dzi_quant(0, 1)
+            dw(1, "ss")
+            finish(0, 0, 2)
+            dzi_quant(1, 1)
+            dw(0, "ss")
+            dt_mm(0, 0, LO)
+            dw(6, "ss")
+            dzT_quant(1, 1)
+            dt_mm(1, 0, LO)
+            finish(0, 0, 0)
+            dw(5, "ss")
+            dt_mm(0, 1, HI)
+            finish(1, 0, 0)
+            dw(7, "ss")
+            dw(3, "ss")
+            finish(0, 1, 2)
+            dt_mm(1, 1, HI)
+            finish(1, 1, 2)
+            dt_mm(1, 1, LO)
+            dw(2, "ss")
+            finish(1, 1, 0)
+            dw(4, "ss")
+            dt_mm(1, 0, HI)
+            finish(1, 0, 2)

@@ -36,6 +36,7 @@ def tile_inimnetdisc_pc_v_kernel(tc, x, w_j, b_j, w_i, phi, grad_out, out_0, out
         id16 = const.tile([P, P], BF16, name="id16")
         make_identity(nc, id32[:])
         make_identity(nc, id16[:])
+        tiny = const.tile([P, 8], BF16, name="tiny")
         warm = const.tile([P, 8], F32, name="warm")
         nc.vector.memset(warm[:], 0.0)
 
@@ -182,6 +183,9 @@ def tile_inimnetdisc_pc_v_kernel(tc, x, w_j, b_j, w_i, phi, grad_out, out_0, out
                 for j in js:
                     nc.vector.tensor_tensor(out=phr[g, h][:, j, :], in0=dh[g, h, j][:], in1=phr[g, h][:, j, :], op=ALU.mult)
 
+            def gate(g, h):
+                nc.gpsimd.tensor_copy(out=tiny[:], in_=dzb[g, h][:, 0, 0:8])
+
             dzTb, dzib = {}, {}
 
             def dz_turn(g, h, engs):
@@ -264,135 +268,139 @@ def tile_inimnetdisc_pc_v_kernel(tc, x, w_j, b_j, w_i, phi, grad_out, out_0, out
 
             LO, HI = (0, 1), (2, 3)
             nc.scalar.activation(warm[:, 0:1], warm[:, 1:2], ACT.Tanh)
-            load_wi(1, 0)
-            wi_group(1, 0, "v")
             load_g(0)
-            g_turn(0, 0, "ss")
-            g_turn(0, 1, "ss")
-            load_wi(0, 0)
-            wi_quant(1, 0)
-            wi_group(0, 0, "v")
-            g_quant(0, 0)
-            wi_quant(0, 0)
-            g_quant(0, 1)
             load_x(0, 0)
-            load_wi(0, 1)
-            wi_group(0, 1, "v")
-            tanh(0, 0)
-            square(0, 0, LO)
-            load_wi(1, 1)
-            wi_group(1, 1, "v")
-            wi_quant(0, 1)
-            dh_mm(0, 0, LO)
-            load_x(1, 0)
-            load_phi(0, 0)
-            wi_quant(1, 1)
-            dh_mm(0, 0, HI)
+            t_group(0, 0)
+            load_wi(0, 0)
+            g_turn(0, 0, "vv")
+            g_quant(0, 0)
+            g_turn(0, 1, "vv")
+            wi_group(0, 0, "v")
             load_g(1)
+            load_wi(0, 1)
+            load_x(1, 0)
+            t_quant(0, 0)
+            tanh(0, 0)
+            g_turn(1, 0, "vs")
+            wi_group(0, 1, "v")
+            square(0, 0, LO)
+            g_quant(0, 1)
+            g_turn(1, 1, "ss")
+            load_wi(1, 0)
+            load_wi(1, 1)
+            wi_quant(0, 1)
+            wi_quant(0, 0)
+            dh_mm(0, 0, LO)
+            wi_group(1, 0, "v")
+            g_quant(1, 0)
+            g_quant(1, 1)
             dz(0, 0, LO)
             square(0, 0, HI)
-            a(0, 0, HI, "v")
-            dz(0, 0, HI)
+            wi_quant(1, 0)
             tanh(1, 0)
-            a(0, 0, LO, "v")
+            dh_mm(0, 0, HI)
+            dz(0, 0, HI)
+            t_group(1, 0)
+            load_phi(0, 0)
+            a(0, 0, LO, "g")
+            dz_turn(0, 0, "vv")
+            a(0, 0, HI, "g")
+            dh_mm(1, 0, LO)
+            wi_group(1, 1, "s")
+            u(0, 0, LO)
             square(1, 0, LO)
             square(1, 0, HI)
-            load_x(0, 1)
-            g_turn(1, 0, "ss")
-            load_phi(1, 0)
-            load_phi(0, 1)
-            tanh(0, 1)
-            u(0, 0, LO)
-            g_turn(1, 1, "ss")
-            g_quant(1, 0)
-            load_phi(1, 1)
-            t_group(1, 0)
-            dz_turn(0, 0, "ss")
-            a(1, 0, HI, "v")
             u(0, 0, HI)
-            a(0, 1, LO, "v")
-            g_quant(1, 1)
-            load_x(1, 1)
-            a(1, 0, LO, "v")
-            tanh(1, 1)
-            dh_mm(1, 0, LO)
-            dz_group(0, 0, "ss")
-            load_wj(1)
-            dh_mm(0, 1, LO)
-            a(0, 1, HI, "v")
-            u(1, 0, LO)
-            load_wj(0)
-            dz(1, 0, LO)
-            dh_mm(1, 0, HI)
-            dz(1, 0, HI)
-            a(1, 1, HI, "v")
-            dzi_quant(0, 0)
-            square(0, 1, LO)
-            wj_group(1, 1, "ss")
-            square(1, 1, LO)
-            dz_turn(1, 0, "ss")
-            square(0, 1, HI)
-            u(1, 0, HI)
-            u(0, 1, LO)
+            load_phi(1, 0)
+            wi_quant(1, 1)
+            gate(0, 0)
             t_quant(1, 0)
+            load_x(0, 1)
+            dz(1, 0, LO)
+            dz_group(0, 0, "vs")
+            tanh(0, 1)
+            load_x(1, 1)
+            dh_mm(1, 0, HI)
+            square(0, 1, LO)
+            dz(1, 0, HI)
+            dzi_quant(0, 0)
+            dz_turn(1, 0, "sv")
+            a(1, 0, LO, "g")
             dzT_quant(0, 0)
-            dz(0, 1, LO)
-            dz_group(1, 0, "ss")
-            dh_mm(0, 1, HI)
-            t_group(1, 1)
-            a(1, 1, LO, "v")
-            wj_group(0, 1, "ss")
-            dzT_quant(1, 0)
-            dz(0, 1, HI)
-            t_quant(1, 1)
-            dzi_quant(1, 0)
-            u(0, 1, HI)
-            wj_quant(1, 1)
-            dh_mm(1, 1, LO)
-            u(1, 1, LO)
-            square(1, 1, HI)
-            dh_mm(1, 1, HI)
-            u(1, 1, HI)
+            u(1, 0, LO)
             t_group(0, 1)
-            dz_turn(0, 1, "ss")
-            dz_group(0, 1, "ss")
-            wj_group(0, 0, "ss")
-            dz(1, 1, LO)
-            dzT_quant(0, 1)
-            wj_group(1, 0, "ss")
-            wj_quant(0, 1)
-            dt_mm(0, 1, LO)
-            t_group(0, 0)
+            dh_mm(0, 1, LO)
+            dz(0, 1, LO)
+            a(1, 0, HI, "g")
+            gate(1, 0)
+            u(1, 0, HI)
+            dz_group(1, 0, "vs")
+            load_phi(1, 1)
+            square(0, 1, HI)
+            load_wj(1)
+            load_phi(0, 1)
+            gate(0, 1)
+            t_group(1, 1)
+            dh_mm(0, 1, HI)
+            dh_mm(1, 1, HI)
+            a(0, 1, LO, "g")
+            dz(0, 1, HI)
+            dz_turn(0, 1, "vs")
+            tanh(1, 1)
+            dzT_quant(1, 0)
+            u(0, 1, LO)
+            a(0, 1, HI, "g")
+            dz_group(0, 1, "vv")
+            load_wj(0)
+            square(1, 1, LO)
+            wj_group(1, 1, "ss")
             t_quant(0, 1)
-            wj_quant(0, 0)
+            u(0, 1, HI)
+            dh_mm(1, 1, LO)
+            dzT_quant(0, 1)
+            dzi_quant(1, 0)
+            a(1, 1, LO, "g")
+            square(1, 1, HI)
+            dz(1, 1, LO)
+            wj_group(0, 0, "ss")
+            wj_group(1, 0, "ss")
             dz(1, 1, HI)
-            dz_group(1, 1, "ss")
-            wj_quant(1, 0)
-            finish(0, 1, 0)
-            dt_mm(0, 0, HI)
-            dz_turn(1, 1, "ss")
-            t_quant(0, 0)
+            t_quant(1, 1)
             dzi_quant(0, 1)
-            dw(1, "ss")
-            finish(0, 0, 2)
+            wj_quant(0, 0)
+            wj_quant(1, 0)
+            dz_group(1, 1, "ss")
+            dz_turn(1, 1, "ss")
+            u(1, 1, LO)
+            a(1, 1, HI, "g")
+            u(1, 1, HI)
             dzi_quant(1, 1)
-            dw(0, "ss")
-            dt_mm(0, 0, LO)
-            dw(6, "ss")
+            dt_mm(0, 0, HI)
+            wj_group(0, 1, "ss")
+            gate(1, 1)
             dzT_quant(1, 1)
-            dt_mm(1, 0, LO)
-            finish(0, 0, 0)
-            dw(5, "ss")
-            dt_mm(0, 1, HI)
-            finish(1, 0, 0)
-            dw(7, "ss")
-            dw(3, "ss")
-            finish(0, 1, 2)
-            dt_mm(1, 1, HI)
-            finish(1, 1, 2)
-            dt_mm(1, 1, LO)
-            dw(2, "ss")
-            finish(1, 1, 0)
-            dw(4, "ss")
             dt_mm(1, 0, HI)
+            finish(0, 0, 2)
+            dw(1, "ss")
             finish(1, 0, 2)
+            wj_quant(0, 1)
+            dt_mm(1, 0, LO)
+            dw(7, "ss")
+            wj_quant(1, 1)
+            dw(3, "ss")
+            finish(1, 0, 0)
+            dt_mm(0, 0, LO)
+            dw(4, "ss")
+            finish(0, 0, 0)
+            dt_mm(1, 1, HI)
+            dw(2, "ss")
+            dt_mm(1, 1, LO)
+            finish(1, 1, 2)
+            dw(5, "ss")
+            dw(6, "ss")
+            finish(1, 1, 0)
+            dt_mm(0, 1, HI)
+            dw(0, "ss")
+            finish(0, 1, 2)
+            dt_mm(0, 1, LO)
+            finish(0, 1, 0)

@@ -201,9 +201,9 @@ def tile_inimnetdisc_pc_v_kernel(tc, x, w_j, b_j, w_i, phi, grad_out, out_0, out
                     for k in range(2):
                         w0 = b * 256 + k * P
                         nc.tensor.matmul(
-                            bank[:, k * P : (k + 1) * P, :],
+                            bank[:, k * P : (k + 1) * P, :].rearrange("p (c i) j -> p c j i", i=4),
                             lhsT=id16[:],
-                            rhs=src[:, :, w0 : w0 + P].rearrange("p j w -> p w j"),
+                            rhs=src[:, :, w0 : w0 + P].rearrange("p j (c i) -> p c j i", i=4),
                             start=True,
                             stop=True,
                         )

@@ -68,9 +68,10 @@ def tile_inimnetdisc_pc_v_kernel(tc, x, w_j, b_j, w_i, phi, grad_out, out_0, out
         with tc.manual_schedule():
             xr, phr, s, t32, dzb = {}, {}, {}, {}, {}
 
-            def load_x(g, h):
-                xr[g, h] = keep.tile([P, J, H], BF16, name=f"x{g}{h}")
-                nc.sync.dma_start(out=xr[g, h][:], in_=x_v[g][:, :, half(h)])
+            def load_x(g, b):
+                if b == 0:
+                    xr[g] = keep.tile([P, J, D], BF16, name=f"x{g}")
+                nc.sync.dma_start(out=xr[g][:, 2 * b : 2 * b + 2], in_=x_v[g][:, 2 * b : 2 * b + 2])
 
             def load_phi(g, h):
                 phr[g, h] = keep.tile([P, J, H], F32, name=f"phi{g}{h}")
@@ -83,17 +84,20 @@ def tile_inimnetdisc_pc_v_kernel(tc, x, w_j, b_j, w_i, phi, grad_out, out_0, out
                     wir[h] = raw.tile([P, 2, J, H], BF16, name="rawt")
                 nc.sync.dma_start(out=wir[h][:, c], in_=wi_v[c][:, :, half(h)])
 
-            def load_g(g):
-                gr[g] = raw.tile([P, J, D], BF16, name="rawt")
-                nc.sync.dma_start(out=gr[g][:], in_=go_v[g])
+            def load_g(g, b):
+                if b == 0:
+                    gr[g] = raw.tile([P, J, D], BF16, name="rawt")
+                nc.sync.dma_start(out=gr[g][:, 2 * b : 2 * b + 2], in_=go_v[g][:, 2 * b : 2 * b + 2])
 
             def load_wj(c):
                 wjr[c] = raw.tile([P, J, D], BF16, name="rawt")
                 nc.sync.dma_start(out=wjr[c][:], in_=wj_v[c])
 
-            def tanh(g, h):
-                t32[g, h] = work.tile([P, J, H], F32, name="t32", bufs=2)
-                nc.scalar.activation(t32[g, h][:], xr[g, h][:], ACT.Tanh)
+            def tanh(g, h, b):
+                if b == 0:
+                    t32[g, h] = work.tile([P, J, H], F32, name="t32", bufs=2)
+                jj = slice(2 * b, 2 * b + 2)
+                nc.scalar.activation(t32[g, h][:, jj], xr[g][:, jj, half(h)], ACT.Tanh)
 
             def square(g, h, js):
                 if js[0] == 0:
@@ -110,7 +114,7 @@ def tile_inimnetdisc_pc_v_kernel(tc, x, w_j, b_j, w_i, phi, grad_out, out_0, out
 
             def t_group(g, h):
                 tb[g, h] = grouped()
-                nc.scalar.activation(tb[g, h][:], xr[g, h][:].rearrange("p j w -> p w j"), ACT.Tanh)
+                nc.scalar.activation(tb[g, h][:], xr[g][:, :, half(h)].rearrange("p j w -> p w j"), ACT.Tanh)
 
             def t_quant(g, h):
                 quant(t_q, g, half(h), flat(tb[g, h]), E4M3)
@@ -132,27 +136,23 @@ def tile_inimnetdisc_pc_v_kernel(tc, x, w_j, b_j, w_i, phi, grad_out, out_0, out
 
             gt = {}
 
-            def transposes(src32, col0):
-                banks = []
-                for b in range(2):
-                    bank = psum.tile([P, 2, 2, P], F32, name="tr", bufs=2)
-                    for jj in range(2):
-                        for u in range(2):
-                            nc.tensor.transpose(bank[:, jj, u, :], src32[:, 2 * b + jj, col0 + u : col0 + 2 * P : 2], id32[:])
-                    banks.append(bank)
-                return banks
+            def transposes(src32, col0, b):
+                bank = psum.tile([P, 2, 2, P], F32, name="tr", bufs=2)
+                for jj in range(2):
+                    for u in range(2):
+                        nc.tensor.transpose(bank[:, jj, u, :], src32[:, 2 * b + jj, col0 + u : col0 + 2 * P : 2], id32[:])
+                return bank
 
             def untranspose(eng, dst, bank, b):
                 o = dst[:].rearrange("p w j -> p (w j)").bitcast(F32).rearrange("p (b a r u) -> p b a r u", b=2, a=2, u=2)[:, b]
                 i = bank[:].rearrange("p a u r -> p a r u")
                 copier(eng)(out=o, in_=i)
 
-            def g_turn(g, c, engs):
-                gt[g, c] = grouped()
+            def g_turn(g, c, b, eng):
+                if b == 0:
+                    gt[g, c] = grouped()
                 words = gr[g][:].rearrange("p j w -> p (j w)").bitcast(F32).rearrange("p (j w) -> p j w", j=J)
-                banks = transposes(words, 256 * c)
-                for b in range(2):
-                    untranspose(engs[b], gt[g, c], banks[b], b)
+                untranspose(eng, gt[g, c], transposes(words, 256 * c, b), b)
 
             def g_quant(g, c):
                 quant(g_q, c, half(g), flat(gt[g, c]), E5M2)
@@ -188,30 +188,26 @@ def tile_inimnetdisc_pc_v_kernel(tc, x, w_j, b_j, w_i, phi, grad_out, out_0, out
 
             dzTb, dzib = {}, {}
 
-            def dz_turn(g, h, engs):
-                dzTb[g, h] = grouped()
+            def dz_turn(g, h, b, eng):
+                if b == 0:
+                    dzTb[g, h] = grouped()
                 words = dzb[g, h][:].rearrange("p j w -> p (j w)").bitcast(F32).rearrange("p (j w) -> p j w", j=J)
-                banks = transposes(words, 0)
-                for b in range(2):
-                    untranspose(engs[b], dzTb[g, h], banks[b], b)
+                untranspose(eng, dzTb[g, h], transposes(words, 0, b), b)
 
-            def move(dst, src, engs):
-                for b in range(2):
-                    bank = psum.tile([P, 2 * P, J], BF16, name="tr", bufs=2)
-                    for k in range(2):
-                        w0 = b * 256 + k * P
-                        nc.tensor.matmul(
-                            bank[:, k * P : (k + 1) * P, :].rearrange("p (c i) j -> p c j i", i=4),
-                            lhsT=id16[:],
-                            rhs=src[:, :, w0 : w0 + P].rearrange("p j (c i) -> p c j i", i=4),
-                            start=True,
-                            stop=True,
-                        )
-                    copier(engs[b])(out=dst[:, b * 256 : b * 256 + 256, :], in_=bank[:])
-
-            def dz_group(g, h, engs):
-                dzib[g, h] = grouped()
-                move(dzib[g, h], dzb[g, h], engs)
+            def dz_group(g, h, b, eng):
+                if b == 0:
+                    dzib[g, h] = grouped()
+                bank = psum.tile([P, 2 * P, J], BF16, name="tr", bufs=2)
+                for k in range(2):
+                    w0 = b * 256 + k * P
+                    nc.tensor.matmul(
+                        bank[:, k * P : (k + 1) * P, :].rearrange("p (c i) j -> p c j i", i=4),
+                        lhsT=id16[:],
+                        rhs=dzb[g, h][:, :, w0 : w0 + P].rearrange("p j (c i) -> p c j i", i=4),
+                        start=True,
+                        stop=True,
+                    )
+                copier(eng)(out=dzib[g, h][:, b * 256 : b * 256 + 256, :], in_=bank[:])
 
             def dzT_quant(g, h):
                 quant(dzh_q, h, half(g), flat(dzTb[g, h]), E5M2)
@@ -223,7 +219,10 @@ def tile_inimnetdisc_pc_v_kernel(tc, x, w_j, b_j, w_i, phi, grad_out, out_0, out
 
             def wj_group(c, h, engs):
                 wjb[c, h] = grouped()
-                move(wjb[c, h], wjr[c][:, :, half(h)], engs)
+                copier(engs)(
+                    out=wjb[c, h][:].rearrange("p (c i) t -> p c t i", i=4),
+                    in_=wjr[c][:, :, half(h)].rearrange("p t (c i) -> p c t i", i=4),
+                )
 
             def wj_quant(c, h):
                 quant(wj_q, c, half(h), flat(wjb[c, h]), E4M3)
@@ -247,160 +246,236 @@ def tile_inimnetdisc_pc_v_kernel(tc, x, w_j, b_j, w_i, phi, grad_out, out_0, out
                     out=phr[g, h][:, j, :], in0=s[g, h][:, j, :], scalar=1.0, in1=phr[g, h][:, j, :], op0=ALU.subtract, op1=ALU.mult
                 )
 
-            def finish(g, h, j0):
-                v(g, h, j0)
-                v(g, h, j0 + 1)
-                o(g, h, j0)
-                o(g, h, j0 + 1)
+            def gm(g, h, j):
+                nc.scalar.activation(s[g, h][:, j, :], s[g, h][:, j, :], ACT.Copy, bias=-1.0)
+
+            def og(g, h, j):
+                nc.gpsimd.tensor_tensor(out=phr[g, h][:, j, :], in0=s[g, h][:, j, :], in1=phr[g, h][:, j, :], op=ALU.mult)
+
+            def store(g, h, j0):
                 nc.sync.dma_start(out=dx_v[g][:, j0 : j0 + 2, half(h)], in_=phr[g, h][:, j0 : j0 + 2, :])
 
-            def dw(m, engs):
-                stage = work.tile([P, D], F32, name="dw", bufs=3)
-                for h in range(2):
-                    bank = psum.tile([P, H], F32, name="acc", bufs=6)
-                    for g in range(2):
-                        mx(bank[:], dzt_q, g, m * P, E5M2, t_q, g, h * H, E4M3, g == 0, g == 1)
-                    if engs[h] == "s":
-                        nc.scalar.activation(stage[:, half(h)], bank[:], ACT.Copy, scale=-1.0)
-                    else:
-                        nc.vector.tensor_scalar(out=stage[:, half(h)], in0=bank[:], scalar1=-1.0, scalar2=None, op0=ALU.mult)
-                nc.sync.dma_start(out=out_1[m * P : (m + 1) * P, :], in_=stage[:])
+            dws = {}
+
+            def dw(m, h, eng):
+                if h == 0:
+                    dws[m] = work.tile([P, D], F32, name="dw", bufs=3)
+                bank = psum.tile([P, H], F32, name="acc", bufs=6)
+                for g in range(2):
+                    mx(bank[:], dzt_q, g, m * P, E5M2, t_q, g, h * H, E4M3, g == 0, g == 1)
+                if eng == "s":
+                    nc.scalar.activation(dws[m][:, half(h)], bank[:], ACT.Copy, scale=-1.0)
+                else:
+                    nc.vector.tensor_scalar(out=dws[m][:, half(h)], in0=bank[:], scalar1=-1.0, scalar2=None, op0=ALU.mult)
+
+            def store_dw(m):
+                nc.sync.dma_start(out=out_1[m * P : (m + 1) * P, :], in_=dws[m][:])
 
             LO, HI = (0, 1), (2, 3)
             nc.scalar.activation(warm[:, 0:1], warm[:, 1:2], ACT.Tanh)
-            load_g(0)
             load_x(0, 0)
-            t_group(0, 0)
-            load_wi(0, 0)
-            g_turn(0, 0, "vv")
-            g_quant(0, 0)
-            g_turn(0, 1, "vv")
-            wi_group(0, 0, "v")
-            load_g(1)
-            load_wi(0, 1)
-            load_x(1, 0)
-            t_quant(0, 0)
-            tanh(0, 0)
-            g_turn(1, 0, "vs")
-            wi_group(0, 1, "v")
-            square(0, 0, LO)
-            g_quant(0, 1)
-            g_turn(1, 1, "ss")
-            load_wi(1, 0)
-            load_wi(1, 1)
-            wi_quant(0, 1)
-            wi_quant(0, 0)
-            dh_mm(0, 0, LO)
-            wi_group(1, 0, "v")
-            g_quant(1, 0)
-            g_quant(1, 1)
-            dz(0, 0, LO)
-            square(0, 0, HI)
-            wi_quant(1, 0)
-            tanh(1, 0)
-            dh_mm(0, 0, HI)
-            dz(0, 0, HI)
-            t_group(1, 0)
-            load_phi(0, 0)
-            a(0, 0, LO, "g")
-            dz_turn(0, 0, "vv")
-            a(0, 0, HI, "g")
-            dh_mm(1, 0, LO)
-            wi_group(1, 1, "s")
-            u(0, 0, LO)
-            square(1, 0, LO)
-            square(1, 0, HI)
-            u(0, 0, HI)
-            load_phi(1, 0)
-            wi_quant(1, 1)
-            gate(0, 0)
-            t_quant(1, 0)
             load_x(0, 1)
-            dz(1, 0, LO)
-            dz_group(0, 0, "vs")
-            tanh(0, 1)
-            load_x(1, 1)
-            dh_mm(1, 0, HI)
-            square(0, 1, LO)
-            dz(1, 0, HI)
-            dzi_quant(0, 0)
-            dz_turn(1, 0, "sv")
-            a(1, 0, LO, "g")
-            dzT_quant(0, 0)
-            u(1, 0, LO)
+            tanh(0, 0, 0)
+            load_wi(0, 0)
+            wi_group(0, 0, "v")
+            wi_quant(0, 0)
+            load_g(0, 0)
+            load_g(0, 1)
+            g_turn(0, 0, 0, "v")
+            square(0, 0, LO)
+            t_group(0, 0)
+            load_wi(0, 1)
+            t_quant(0, 0)
             t_group(0, 1)
-            dh_mm(0, 1, LO)
-            dz(0, 1, LO)
-            a(1, 0, HI, "g")
-            gate(1, 0)
-            u(1, 0, HI)
-            dz_group(1, 0, "vs")
-            load_phi(1, 1)
-            square(0, 1, HI)
-            load_wj(1)
-            load_phi(0, 1)
-            gate(0, 1)
-            t_group(1, 1)
-            dh_mm(0, 1, HI)
-            dh_mm(1, 1, HI)
-            a(0, 1, LO, "g")
-            dz(0, 1, HI)
-            dz_turn(0, 1, "vs")
-            tanh(1, 1)
-            dzT_quant(1, 0)
-            u(0, 1, LO)
-            a(0, 1, HI, "g")
-            dz_group(0, 1, "vv")
-            load_wj(0)
-            square(1, 1, LO)
-            wj_group(1, 1, "ss")
+            g_turn(0, 1, 0, "v")
+            g_turn(0, 0, 1, "s")
+            wi_group(0, 1, "v")
+            g_turn(0, 1, 1, "s")
+            load_g(1, 0)
             t_quant(0, 1)
-            u(0, 1, HI)
+            g_quant(0, 0)
+            tanh(0, 0, 1)
+            square(0, 0, HI)
+            g_turn(1, 0, 0, "s")
+            load_phi(0, 0)
+            load_x(1, 0)
+            load_x(1, 1)
+            load_g(1, 1)
+            g_quant(0, 1)
+            wi_quant(0, 1)
+            tanh(1, 0, 0)
+            load_wi(1, 0)
+            g_turn(1, 1, 0, "v")
+            dh_mm(0, 0, LO)
+            dh_mm(0, 0, HI)
+            dz(0, 0, LO)
+            dz(0, 0, HI)
+            square(1, 0, LO)
+            a(0, 0, LO, "g")
+            u(0, 0, LO)
+            a(0, 0, HI, "g")
+            tanh(1, 0, 1)
+            load_wi(1, 1)
+            dz_turn(0, 0, 0, "v")
+            wi_group(1, 0, "v")
+            g_turn(1, 0, 1, "s")
+            g_quant(1, 0)
+            square(1, 0, HI)
+            wi_group(1, 1, "v")
+            load_phi(1, 0)
+            g_turn(1, 1, 1, "s")
+            g_quant(1, 1)
+            tanh(0, 1, 0)
+            dz_turn(0, 0, 1, "s")
+            a(1, 0, HI, "g")
+            dz_group(0, 0, 0, "s")
+            dh_mm(1, 0, LO)
+            wi_quant(1, 0)
+            wi_quant(1, 1)
+            dh_mm(1, 0, HI)
+            dzT_quant(0, 0)
+            u(0, 0, HI)
+            dz(1, 0, LO)
+            dh_mm(0, 1, LO)
+            gate(0, 0)
+            tanh(0, 1, 1)
+            dz(1, 0, HI)
+            square(0, 1, LO)
+            t_group(1, 0)
+            dz_group(0, 0, 1, "s")
+            square(0, 1, HI)
+            a(1, 0, LO, "g")
+            dz(0, 1, LO)
+            u(1, 0, LO)
+            dz_turn(0, 1, 0, "s")
+            dz_turn(1, 0, 0, "s")
+            u(1, 0, HI)
+            tanh(1, 1, 0)
+            tanh(1, 1, 1)
+            dh_mm(0, 1, HI)
+            dz(0, 1, HI)
+            load_phi(1, 1)
+            load_phi(0, 1)
+            a(0, 1, LO, "g")
+            u(0, 1, LO)
+            load_wj(0)
             dh_mm(1, 1, LO)
+            dz_turn(0, 1, 1, "s")
+            t_quant(1, 0)
             dzT_quant(0, 1)
-            dzi_quant(1, 0)
-            a(1, 1, LO, "g")
+            square(1, 1, LO)
+            dzi_quant(0, 0)
+            wj_group(0, 0, "v")
+            dz_turn(1, 0, 1, "s")
             square(1, 1, HI)
+            dzT_quant(1, 0)
+            load_wj(1)
+            dz_group(1, 0, 0, "s")
+            gate(1, 0)
+            dz_group(1, 0, 1, "s")
+            wj_group(1, 0, "s")
+            a(0, 1, HI, "g")
+            u(0, 1, HI)
+            a(1, 1, LO, "g")
+            dh_mm(1, 1, HI)
+            dz_group(0, 1, 0, "s")
+            a(1, 1, HI, "g")
+            dz_group(0, 1, 1, "s")
+            t_group(1, 1)
             dz(1, 1, LO)
-            wj_group(0, 0, "ss")
-            wj_group(1, 0, "ss")
             dz(1, 1, HI)
-            t_quant(1, 1)
-            dzi_quant(0, 1)
+            u(1, 1, LO)
             wj_quant(0, 0)
             wj_quant(1, 0)
-            dz_group(1, 1, "ss")
-            dz_turn(1, 1, "ss")
-            u(1, 1, LO)
-            a(1, 1, HI, "g")
+            dzi_quant(1, 0)
+            dzi_quant(0, 1)
+            t_quant(1, 1)
+            dz_group(1, 1, 0, "s")
+            dz_group(1, 1, 1, "s")
             u(1, 1, HI)
-            dzi_quant(1, 1)
             dt_mm(0, 0, HI)
-            wj_group(0, 1, "ss")
-            gate(1, 1)
-            dzT_quant(1, 1)
-            dt_mm(1, 0, HI)
-            finish(0, 0, 2)
-            dw(1, "ss")
-            finish(1, 0, 2)
-            wj_quant(0, 1)
-            dt_mm(1, 0, LO)
-            dw(7, "ss")
-            wj_quant(1, 1)
-            dw(3, "ss")
-            finish(1, 0, 0)
+            v(0, 0, 2)
+            dzi_quant(1, 1)
+            dw(0, 0, "s")
+            o(0, 0, 2)
+            v(0, 0, 3)
+            dw(0, 1, "s")
+            store_dw(0)
+            wj_group(0, 1, "v")
+            gm(0, 0, 3)
+            gate(0, 1)
+            dz_turn(1, 1, 0, "s")
+            dz_turn(1, 1, 1, "s")
+            dw(2, 0, "s")
+            dw(2, 1, "s")
+            dw(3, 0, "s")
+            dw(3, 1, "s")
             dt_mm(0, 0, LO)
-            dw(4, "ss")
-            finish(0, 0, 0)
+            wj_group(1, 1, "s")
+            dzT_quant(1, 1)
+            dw(5, 0, "s")
+            wj_quant(0, 1)
+            store_dw(2)
+            v(0, 0, 1)
+            v(0, 0, 0)
+            store_dw(3)
+            o(0, 0, 1)
+            gate(1, 1)
+            og(0, 0, 3)
+            dw(5, 1, "s")
+            dt_mm(1, 0, HI)
+            o(0, 0, 0)
+            dw(4, 0, "s")
+            wj_quant(1, 1)
+            v(1, 0, 2)
+            store(0, 0, 2)
+            v(1, 0, 3)
+            gm(1, 0, 3)
+            dw(4, 1, "s")
+            store(0, 0, 0)
+            o(1, 0, 2)
+            og(1, 0, 3)
+            store_dw(5)
+            store_dw(4)
+            dw(7, 0, "s")
+            dw(7, 1, "s")
             dt_mm(1, 1, HI)
-            dw(2, "ss")
-            dt_mm(1, 1, LO)
-            finish(1, 1, 2)
-            dw(5, "ss")
-            dw(6, "ss")
-            finish(1, 1, 0)
-            dt_mm(0, 1, HI)
-            dw(0, "ss")
-            finish(0, 1, 2)
+            store(1, 0, 2)
+            v(1, 1, 2)
+            gm(1, 1, 3)
+            store_dw(7)
             dt_mm(0, 1, LO)
-            finish(0, 1, 0)
+            gm(0, 1, 3)
+            v(1, 1, 3)
+            dt_mm(0, 1, HI)
+            o(1, 1, 2)
+            v(0, 1, 1)
+            dw(6, 0, "s")
+            dw(6, 1, "s")
+            v(0, 1, 0)
+            v(0, 1, 2)
+            v(0, 1, 3)
+            o(0, 1, 1)
+            o(0, 1, 0)
+            dw(1, 0, "s")
+            og(1, 1, 3)
+            store(1, 1, 2)
+            o(0, 1, 2)
+            dw(1, 1, "s")
+            store_dw(6)
+            dt_mm(1, 1, LO)
+            v(1, 1, 1)
+            og(0, 1, 3)
+            dt_mm(1, 0, LO)
+            v(1, 0, 0)
+            store(0, 1, 0)
+            v(1, 1, 0)
+            v(1, 0, 1)
+            o(1, 0, 0)
+            store(0, 1, 2)
+            store_dw(1)
+            o(1, 0, 1)
+            o(1, 1, 0)
+            store(1, 0, 0)
+            o(1, 1, 1)
+            store(1, 1, 0)

from contextlib import ExitStack

import concourse.mybir as mybir
from concourse.masks import make_identity

F32 = mybir.dt.float32
BF16 = mybir.dt.bfloat16
U32 = mybir.dt.uint32
U8 = mybir.dt.uint8
E4M3 = mybir.dt.float8_e4m3fn_x4
E5M2 = mybir.dt.float8_e5m2_x4
ALU = mybir.AluOpType
ACT = mybir.ActivationFunctionType

FLOPS = 3 * 2 * 1024**3
BYTES = 1024 * 1024 * (4 * 2 + 4 + 2 * 4)

P = 128
J = 4
H = 512
D = 1024


def tile_inimnetdisc_pc_v_kernel(tc, x, w_j, b_j, w_i, phi, grad_out, out_0, out_1):
    nc = tc.nc
    rows = lambda ap: ap.rearrange("(g p j) w -> g p j w", p=P, j=J)
    x_v, wj_v, wi_v, phi_v, go_v, dx_v = rows(x), rows(w_j), rows(w_i), rows(phi), rows(grad_out), rows(out_0)
    with ExitStack() as ctx:
        const = ctx.enter_context(tc.tile_pool(name="const", bufs=1))
        keep = ctx.enter_context(tc.tile_pool(name="keep", bufs=1))
        raw = ctx.enter_context(tc.tile_pool(name="raw", bufs=4))
        work = ctx.enter_context(tc.tile_pool(name="work", bufs=6))
        psum = ctx.enter_context(tc.psum_pool(name="psum", bufs=2))

        id32 = const.tile([P, P], F32, name="id32")
        id16 = const.tile([P, P], BF16, name="id16")
        make_identity(nc, id32[:])
        make_identity(nc, id16[:])
        tiny = const.tile([P, 8], BF16, name="tiny")
        warm = const.tile([P, 8], F32, name="warm")
        nc.vector.memset(warm[:], 0.0)

        def operand(name):
            codes = keep.tile([P, 2, D], U32, name=name + "_c", align_bytes=64)
            scales = keep.tile([P, 2, D], U8, name=name + "_s", align_bytes=64)
            return codes, scales

        wi_q, wj_q, t_q = operand("wi"), operand("wj"), operand("t")
        g_q, dzh_q, dzt_q = operand("g"), operand("dzh"), operand("dzt")

        def quant(dst, c, cols, src, fmt):
            nc.vector.quantize_mx(out=dst[0][:, c, cols].bitcast(fmt), scales=dst[1][:, c, cols], in_=src)

        def mx(out, lhs, c, m0, fl, rhs, cr, n0, fr, start, stop):
            nc.tensor.matmul_mx(
                out=out,
                lhsT=lhs[0][:, c, m0 : m0 + P].bitcast(fl),
                lhsT_scale=lhs[1][:, c, m0 : m0 + P],
                rhs=rhs[0][:, cr, n0 : n0 + H].bitcast(fr),
                rhs_scale=rhs[1][:, cr, n0 : n0 + H],
                start=start,
                stop=stop,
            )

        def half(i):
            return slice(i * H, (i + 1) * H)

        with tc.manual_schedule():
            xr, phr, s, t32, dzb = {}, {}, {}, {}, {}

            def load_x(g, b):
                if b == 0:
                    xr[g] = keep.tile([P, J, D], BF16, name=f"x{g}")
                nc.sync.dma_start(out=xr[g][:, 2 * b : 2 * b + 2], in_=x_v[g][:, 2 * b : 2 * b + 2])

            def load_phi(g, h):
                phr[g, h] = keep.tile([P, J, H], F32, name=f"phi{g}{h}")
                nc.sync.dma_start(out=phr[g, h][:], in_=phi_v[g][:, :, half(h)])

            wir, wjr, gr = {}, {}, {}

            def load_wi(h, c):
                if c == 0:
                    wir[h] = raw.tile([P, 2, J, H], BF16, name="rawt")
                nc.sync.dma_start(out=wir[h][:, c], in_=wi_v[c][:, :, half(h)])

            def load_g(g, b):
                if b == 0:
                    gr[g] = raw.tile([P, J, D], BF16, name="rawt")
                nc.sync.dma_start(out=gr[g][:, 2 * b : 2 * b + 2], in_=go_v[g][:, 2 * b : 2 * b + 2])

            def load_wj(c):
                wjr[c] = raw.tile([P, J, D], BF16, name="rawt")
                nc.sync.dma_start(out=wjr[c][:], in_=wj_v[c])

            def tanh(g, h, b):
                if b == 0:
                    t32[g, h] = work.tile([P, J, H], F32, name="t32", bufs=2)
                jj = slice(2 * b, 2 * b + 2)
                nc.scalar.activation(t32[g, h][:, jj], xr[g][:, jj, half(h)], ACT.Tanh)

            def square(g, h, js):
                if js[0] == 0:
                    s[g, h] = keep.tile([P, J, H], F32, name=f"s{g}{h}")
                nc.scalar.activation(s[g, h][:, js[0] : js[-1] + 1], t32[g, h][:, js[0] : js[-1] + 1], ACT.Square)

            def grouped():
                return work.tile([P, H, J], BF16, name="grouped", align_bytes=64)

            def flat(t):
                return t[:].rearrange("p w j -> p (w j)")

            tb = {}

            def t_group(g, h):
                tb[g, h] = grouped()
                nc.scalar.activation(tb[g, h][:], xr[g][:, :, half(h)].rearrange("p j w -> p w j"), ACT.Tanh)

            def t_quant(g, h):
                quant(t_q, g, half(h), flat(tb[g, h]), E4M3)

            def copier(eng):
                return nc.vector.tensor_copy if eng == "v" else nc.scalar.copy

            wib = {}

            def wi_group(h, c, eng):
                wib[h, c] = grouped()
                copier(eng)(
                    out=wib[h, c][:].rearrange("p (c i) t -> p c t i", i=4),
                    in_=wir[h][:, c].rearrange("p t (c i) -> p c t i", i=4),
                )

            def wi_quant(h, c):
                quant(wi_q, c, half(h), flat(wib[h, c]), E4M3)

            gt = {}

            def transposes(src32, col0, b):
                bank = psum.tile([P, 2, 2, P], F32, name="tr", bufs=2)
                for jj in range(2):
                    for u in range(2):
                        nc.tensor.transpose(bank[:, jj, u, :], src32[:, 2 * b + jj, col0 + u : col0 + 2 * P : 2], id32[:])
                return bank

            def untranspose(eng, dst, bank, b):
                o = dst[:].rearrange("p w j -> p (w j)").bitcast(F32).rearrange("p (b a r u) -> p b a r u", b=2, a=2, u=2)[:, b]
                i = bank[:].rearrange("p a u r -> p a r u")
                copier(eng)(out=o, in_=i)

            def g_turn(g, c, b, eng):
                if b == 0:
                    gt[g, c] = grouped()
                words = gr[g][:].rearrange("p j w -> p (j w)").bitcast(F32).rearrange("p (j w) -> p j w", j=J)
                untranspose(eng, gt[g, c], transposes(words, 256 * c, b), b)

            def g_quant(g, c):
                quant(g_q, c, half(g), flat(gt[g, c]), E5M2)

            dh = {}

            def dh_mm(g, h, js):
                for j in js:
                    bank = psum.tile([P, H], F32, name="acc", bufs=6)
                    for c in range(2):
                        mx(bank[:], g_q, c, g * H + j * P, E5M2, wi_q, c, h * H, E4M3, c == 0, c == 1)
                    dh[g, h, j] = bank

            def dz(g, h, js):
                if js[0] == 0:
                    dzb[g, h] = work.tile([P, J, H], BF16, name="dz", bufs=2)
                for j in js:
                    nc.vector.scalar_tensor_tensor(
                        out=dzb[g, h][:, j, :], in0=s[g, h][:, j, :], scalar=1.0, in1=dh[g, h, j][:], op0=ALU.subtract, op1=ALU.mult
                    )

            def a(g, h, js, eng):
                for j in js:
                    e = nc.gpsimd if eng == "g" else nc.vector
                    e.tensor_tensor(out=phr[g, h][:, j, :], in0=t32[g, h][:, j, :], in1=phr[g, h][:, j, :], op=ALU.mult)

            def u(g, h, js):
                for j in js:
                    nc.vector.tensor_tensor(out=phr[g, h][:, j, :], in0=dh[g, h, j][:], in1=phr[g, h][:, j, :], op=ALU.mult)

            def gate(g, h):
                nc.gpsimd.tensor_copy(out=tiny[:], in_=dzb[g, h][:, 0, 0:8])

            dzTb, dzib = {}, {}

            def dz_turn(g, h, b, eng):
                if b == 0:
                    dzTb[g, h] = grouped()
                words = dzb[g, h][:].rearrange("p j w -> p (j w)").bitcast(F32).rearrange("p (j w) -> p j w", j=J)
                untranspose(eng, dzTb[g, h], transposes(words, 0, b), b)

            def dz_group(g, h, b, eng):
                if b == 0:
                    dzib[g, h] = grouped()
                bank = psum.tile([P, 2 * P, J], BF16, name="tr", bufs=2)
                for k in range(2):
                    w0 = b * 256 + k * P
                    nc.tensor.matmul(
                        bank[:, k * P : (k + 1) * P, :].rearrange("p (c i) j -> p c j i", i=4),
                        lhsT=id16[:],
                        rhs=dzb[g, h][:, :, w0 : w0 + P].rearrange("p j (c i) -> p c j i", i=4),
                        start=True,
                        stop=True,
                    )
                copier(eng)(out=dzib[g, h][:, b * 256 : b * 256 + 256, :], in_=bank[:])

            def dzT_quant(g, h):
                quant(dzh_q, h, half(g), flat(dzTb[g, h]), E5M2)

            def dzi_quant(g, h):
                quant(dzt_q, g, half(h), flat(dzib[g, h]), E5M2)

            wjb = {}

            def wj_group(c, h, engs):
                wjb[c, h] = grouped()
                copier(engs)(
                    out=wjb[c, h][:].rearrange("p (c i) t -> p c t i", i=4),
                    in_=wjr[c][:, :, half(h)].rearrange("p t (c i) -> p c t i", i=4),
                )

            def wj_quant(c, h):
                quant(wj_q, c, half(h), flat(wjb[c, h]), E4M3)

            dt = {}

            def dt_mm(g, h, js):
                for j in js:
                    bank = psum.tile([P, H], F32, name="acc", bufs=6)
                    for c in range(2):
                        mx(bank[:], dzh_q, c, g * H + j * P, E5M2, wj_q, c, h * H, E4M3, c == 0, c == 1)
                    dt[g, h, j] = bank

            def v(g, h, j):
                nc.vector.scalar_tensor_tensor(
                    out=phr[g, h][:, j, :], in0=phr[g, h][:, j, :], scalar=2.0, in1=dt[g, h, j][:], op0=ALU.mult, op1=ALU.add
                )

            def o(g, h, j):
                nc.vector.scalar_tensor_tensor(
                    out=phr[g, h][:, j, :], in0=s[g, h][:, j, :], scalar=1.0, in1=phr[g, h][:, j, :], op0=ALU.subtract, op1=ALU.mult
                )

            def gm(g, h, j):
                nc.scalar.activation(s[g, h][:, j, :], s[g, h][:, j, :], ACT.Copy, bias=-1.0)

            def og(g, h, j):
                nc.gpsimd.tensor_tensor(out=phr[g, h][:, j, :], in0=s[g, h][:, j, :], in1=phr[g, h][:, j, :], op=ALU.mult)

            def store(g, h, j0):
                nc.sync.dma_start(out=dx_v[g][:, j0 : j0 + 2, half(h)], in_=phr[g, h][:, j0 : j0 + 2, :])

            dws = {}

            def dw(m, h, eng):
                if h == 0:
                    dws[m] = work.tile([P, D], F32, name="dw", bufs=3)
                bank = psum.tile([P, H], F32, name="acc", bufs=6)
                for g in range(2):
                    mx(bank[:], dzt_q, g, m * P, E5M2, t_q, g, h * H, E4M3, g == 0, g == 1)
                if eng == "s":
                    nc.scalar.activation(dws[m][:, half(h)], bank[:], ACT.Copy, scale=-1.0)
                else:
                    nc.vector.tensor_scalar(out=dws[m][:, half(h)], in0=bank[:], scalar1=-1.0, scalar2=None, op0=ALU.mult)

            def store_dw(m):
                nc.sync.dma_start(out=out_1[m * P : (m + 1) * P, :], in_=dws[m][:])

            LO, HI = (0, 1), (2, 3)
            nc.scalar.activation(warm[:, 0:1], warm[:, 1:2], ACT.Tanh)
            load_x(0, 0)
            load_x(0, 1)
            tanh(0, 0, 0)
            load_wi(0, 0)
            wi_group(0, 0, "v")
            wi_quant(0, 0)
            load_g(0, 0)
            load_g(0, 1)
            g_turn(0, 0, 0, "v")
            square(0, 0, LO)
            t_group(0, 0)
            load_wi(0, 1)
            t_quant(0, 0)
            t_group(0, 1)
            g_turn(0, 1, 0, "v")
            g_turn(0, 0, 1, "s")
            wi_group(0, 1, "v")
            g_turn(0, 1, 1, "s")
            load_g(1, 0)
            t_quant(0, 1)
            g_quant(0, 0)
            tanh(0, 0, 1)
            square(0, 0, HI)
            g_turn(1, 0, 0, "s")
            load_phi(0, 0)
            load_x(1, 0)
            load_x(1, 1)
            load_g(1, 1)
            g_quant(0, 1)
            wi_quant(0, 1)
            tanh(1, 0, 0)
            load_wi(1, 0)
            g_turn(1, 1, 0, "v")
            dh_mm(0, 0, LO)
            dh_mm(0, 0, HI)
            dz(0, 0, LO)
            dz(0, 0, HI)
            square(1, 0, LO)
            a(0, 0, LO, "g")
            u(0, 0, LO)
            a(0, 0, HI, "g")
            tanh(1, 0, 1)
            load_wi(1, 1)
            dz_turn(0, 0, 0, "v")
            wi_group(1, 0, "v")
            g_turn(1, 0, 1, "s")
            g_quant(1, 0)
            square(1, 0, HI)
            wi_group(1, 1, "v")
            load_phi(1, 0)
            g_turn(1, 1, 1, "s")
            g_quant(1, 1)
            tanh(0, 1, 0)
            dz_turn(0, 0, 1, "s")
            a(1, 0, HI, "g")
            dz_group(0, 0, 0, "s")
            dh_mm(1, 0, LO)
            wi_quant(1, 0)
            wi_quant(1, 1)
            dh_mm(1, 0, HI)
            dzT_quant(0, 0)
            u(0, 0, HI)
            dz(1, 0, LO)
            dh_mm(0, 1, LO)
            gate(0, 0)
            tanh(0, 1, 1)
            dz(1, 0, HI)
            square(0, 1, LO)
            t_group(1, 0)
            dz_group(0, 0, 1, "s")
            square(0, 1, HI)
            a(1, 0, LO, "g")
            dz(0, 1, LO)
            u(1, 0, LO)
            dz_turn(0, 1, 0, "s")
            dz_turn(1, 0, 0, "s")
            u(1, 0, HI)
            tanh(1, 1, 0)
            tanh(1, 1, 1)
            dh_mm(0, 1, HI)
            dz(0, 1, HI)
            load_phi(1, 1)
            load_phi(0, 1)
            a(0, 1, LO, "g")
            u(0, 1, LO)
            load_wj(0)
            dh_mm(1, 1, LO)
            dz_turn(0, 1, 1, "s")
            t_quant(1, 0)
            dzT_quant(0, 1)
            square(1, 1, LO)
            dzi_quant(0, 0)
            wj_group(0, 0, "v")
            dz_turn(1, 0, 1, "s")
            square(1, 1, HI)
            dzT_quant(1, 0)
            load_wj(1)
            dz_group(1, 0, 0, "s")
            gate(1, 0)
            dz_group(1, 0, 1, "s")
            wj_group(1, 0, "s")
            a(0, 1, HI, "g")
            u(0, 1, HI)
            a(1, 1, LO, "g")
            dh_mm(1, 1, HI)
            dz_group(0, 1, 0, "s")
            a(1, 1, HI, "g")
            dz_group(0, 1, 1, "s")
            t_group(1, 1)
            dz(1, 1, LO)
            dz(1, 1, HI)
            u(1, 1, LO)
            wj_quant(0, 0)
            wj_quant(1, 0)
            dzi_quant(1, 0)
            dzi_quant(0, 1)
            t_quant(1, 1)
            dz_group(1, 1, 0, "s")
            dz_group(1, 1, 1, "s")
            u(1, 1, HI)
            dt_mm(0, 0, HI)
            v(0, 0, 2)
            dzi_quant(1, 1)
            dw(0, 0, "s")
            o(0, 0, 2)
            v(0, 0, 3)
            dw(0, 1, "s")
            store_dw(0)
            wj_group(0, 1, "v")
            gm(0, 0, 3)
            gate(0, 1)
            dz_turn(1, 1, 0, "s")
            dz_turn(1, 1, 1, "s")
            dw(2, 0, "s")
            dw(2, 1, "s")
            dw(3, 0, "s")
            dw(3, 1, "s")
            dt_mm(0, 0, LO)
            wj_group(1, 1, "s")
            dzT_quant(1, 1)
            dw(5, 0, "s")
            wj_quant(0, 1)
            store_dw(2)
            v(0, 0, 1)
            v(0, 0, 0)
            store_dw(3)
            o(0, 0, 1)
            gate(1, 1)
            og(0, 0, 3)
            dw(5, 1, "s")
            dt_mm(1, 0, HI)
            o(0, 0, 0)
            dw(4, 0, "s")
            wj_quant(1, 1)
            v(1, 0, 2)
            store(0, 0, 2)
            v(1, 0, 3)
            gm(1, 0, 3)
            dw(4, 1, "s")
            store(0, 0, 0)
            o(1, 0, 2)
            og(1, 0, 3)
            store_dw(5)
            store_dw(4)
            dw(7, 0, "s")
            dw(7, 1, "s")
            dt_mm(1, 1, HI)
            store(1, 0, 2)
            v(1, 1, 2)
            gm(1, 1, 3)
            store_dw(7)
            dt_mm(0, 1, LO)
            gm(0, 1, 3)
            v(1, 1, 3)
            dt_mm(0, 1, HI)
            o(1, 1, 2)
            v(0, 1, 1)
            dw(6, 0, "s")
            dw(6, 1, "s")
            v(0, 1, 0)
            v(0, 1, 2)
            v(0, 1, 3)
            o(0, 1, 1)
            o(0, 1, 0)
            dw(1, 0, "s")
            og(1, 1, 3)
            store(1, 1, 2)
            o(0, 1, 2)
            dw(1, 1, "s")
            store_dw(6)
            dt_mm(1, 1, LO)
            v(1, 1, 1)
            og(0, 1, 3)
            dt_mm(1, 0, LO)
            v(1, 0, 0)
            store(0, 1, 0)
            v(1, 1, 0)
            v(1, 0, 1)
            o(1, 0, 0)
            store(0, 1, 2)
            store_dw(1)
            o(1, 0, 1)
            o(1, 1, 0)
            store(1, 0, 0)
            o(1, 1, 1)
            store(1, 1, 0)
